import numpy as np
import ml_dtypes


def mxq(x, axis, fmt="e4m3"):
    dtype, down = {"e4m3": (ml_dtypes.float8_e4m3fn, 7), "e5m2": (ml_dtypes.float8_e5m2, 14)}[fmt]
    v = np.moveaxis(np.asarray(x, np.float32).astype(ml_dtypes.bfloat16).astype(np.float64), axis, -1)
    blocks = v.reshape(v.shape[:-1] + (-1, 32))
    amax = np.abs(blocks).max(-1, keepdims=True)
    byte = np.maximum(np.where(amax > 0, np.frexp(amax)[1] - 1 + 127, 0) - down, 1)
    scale = np.exp2(byte - 127.0)
    codes = (blocks / scale).astype(np.float32).astype(dtype).astype(np.float64)
    return np.moveaxis((codes * scale).reshape(v.shape), -1, axis)


WIDE = False


def mx_kscale(k):
    if not WIDE:
        return np.ones(k)
    levels = np.array([10, -10, 5, -5, 0])
    if k % 512:
        return np.exp2(np.random.permutation(np.resize(levels, k // 32))).repeat(32)
    a = np.empty((k // 512, 16))
    for p in range(k // 512):
        a[p, :8] = np.random.permutation(np.resize(levels, 8))
        for g in range(8):
            far = levels[np.abs(levels - a[p, g]) >= 10]
            a[p, g + 8] = far[np.random.randint(len(far))]
    return np.exp2(a.ravel()).repeat(32)


BF16 = ml_dtypes.bfloat16


def bf(x):
    return np.asarray(x, np.float32).astype(BF16)


def f64(x):
    return np.asarray(x).astype(np.float64)


B, D, DO, H, T, P = 1024, 1024, 1024, 256, 8, 2


def setup_inputs():
    s = mx_kscale(D)
    return {"transformed": bf(np.random.standard_normal((B, D)) * 1.2 * s),
            "coeff": bf(np.random.standard_normal((B, P)) * 0.45),
            "task_mats": bf(np.random.standard_normal((P, D, D)) / np.sqrt(D) / s[None, :, None] * s[None, None, :])}


def reference(transformed, coeff, task_mats):
    x, c, m = f64(transformed), f64(coeff), f64(task_mats)
    for j in range(P):
        x = x + c[:, j:j + 1] * (mxq(x, 1, "e4m3") @ mxq(m[j], 0, "e4m3"))
    return x

@@ -1,0 +1,232 @@
+from contextlib import ExitStack
+
+import concourse.mybir as mybir
+from concourse.masks import make_identity
+
+F32 = mybir.dt.float32
+BF16 = mybir.dt.bfloat16
+U32 = mybir.dt.uint32
+U8 = mybir.dt.uint8
+FP8X4 = mybir.dt.float8_e4m3fn_x4
+MULT = mybir.AluOpType.mult
+ADD = mybir.AluOpType.add
+
+P = 128
+NB = 8
+D = 1024
+HALF = 512
+FLOPS = 2 * 2 * 1024 * 1024 * 1024
+
+BANKS = 4
+NV = {(0, 0): 336, (0, 1): 320, (1, 0): 256, (1, 1): 0}
+LOADS = [("x", 0), ("m", 0, 0), ("x", 1), ("m", 0, 1), ("x", 2), ("x", 3), ("m", 1, 0), ("m", 1, 1)]
+GROUPS = [(1, 0, 0), (1, 1, 0), (1, 0, 1), (1, 1, 1), (1, 2, 0), (1, 2, 1), (2, 0, 0), (1, 3, 0), (2, 1, 0), (1, 3, 1), (2, 2, 0), (2, 0, 1), (2, 1, 1), (2, 2, 1), (2, 3, 0), (2, 3, 1)]
+FILL_T = {
+    -1: [0, 1],
+    1: [2],
+    2: [3],
+}
+FILL_S = {
+    -1: [("ex", 0, 0), ("rm", 0, 0, 0), ("ex", 0, 1), ("rm", 0, 0, 1), ("ex", 1, 0), ("rm", 0, 1, 0), ("ex", 1, 1), ("rm", 0, 1, 1)],
+    1: [("ex", 2, 0), ("ex", 2, 1), ("rm", 1, 0, 0)],
+    2: [("rm", 1, 0, 1), ("ex", 3, 0), ("ex", 3, 1)],
+    4: [("rm", 1, 1, 0)],
+    7: [("rm", 1, 1, 1)],
+}
+FILL_V = {
+    -1: [("rm", 0, 0, 0), ("qm", 0, 0, 0), ("rm", 0, 0, 1), ("qx", 0), ("qm", 0, 0, 1), ("rm", 0, 1, 0), ("qm", 0, 1, 0), ("qx", 1), ("rm", 0, 1, 1)],
+    0: [("qm", 0, 1, 1)],
+    1: [("q1", 0, 0)],
+    2: [("rm", 1, 0, 0), ("qx", 2), ("qm", 1, 0, 0)],
+    3: [("rm", 1, 0, 1)],
+    4: [("qx", 3), ("q1", 0, 1), ("qm", 1, 0, 1), ("q1", 1, 0), ("q1", 1, 1)],
+    6: [("qm", 1, 1, 0)],
+    8: [("q1", 2, 0), ("q1", 2, 1)],
+    9: [("qm", 1, 1, 1)],
+    10: [("q1", 3, 0)],
+    12: [("q1", 3, 1)],
+}
+
+
+def tile_precomputedmetanet_pa_kernel(tc, transformed, coeff, task_mats, out):
+    nc = tc.nc
+    xv = transformed.rearrange("(p m) k -> p m k", m=NB)
+    ov = out.rearrange("(p m) n -> p m n", m=NB)
+    with ExitStack() as ctx:
+        keep = ctx.enter_context(tc.tile_pool(name="keep", bufs=1))
+        stage = ctx.enter_context(tc.tile_pool(name="stage", bufs=8))
+        psum = ctx.enter_context(tc.psum_pool(name="psum", bufs=1))
+        ctx.enter_context(tc.manual_schedule())
+
+        ident = keep.tile([P, P], F32, name="ident")
+        make_identity(nc, ident[:])
+        c_bf = keep.tile([P, 2 * NB], BF16, name="c_bf")
+        nc.scalar.dma_start(out=c_bf[:], in_=coeff.rearrange("(p m) j -> p (m j)", m=NB))
+        c32 = keep.tile([P, 2 * NB], F32, name="c32")
+        nc.vector.tensor_copy(out=c32[:], in_=c_bf[:])
+
+        t = {}
+        count = {"tp": 0, "acc": 0}
+
+        def bank(kind):
+            k = count[kind]
+            count[kind] = k + 1
+            return psum.tile([P, HALF], F32, name="%s%d" % (kind, k % BANKS), tag="%s%d" % (kind, k % BANKS))
+
+        def load_x(i):
+            t["xp", i] = keep.tile([P, 2 * D], BF16, name="xp%d" % i)
+            nc.sync.dma_start(
+                out=t["xp", i][:].rearrange("p (m k) -> p m k", m=2), in_=xv[:, 2 * i : 2 * i + 2, :]
+            )
+
+        def load_m(mat, h):
+            raw = keep.tile([P, 8, HALF], BF16, name="raw%d_%d" % (mat, h))
+            t["raw", mat, h] = raw
+            cols = slice(HALF * h, HALF * h + HALF)
+            for g in range(2):
+                nc.sync.dma_start(
+                    out=raw[:, 4 * g : 4 * g + 4, :],
+                    in_=task_mats[mat, 512 * g : 512 * g + 512, cols].rearrange("(p j) c -> p j c", j=4),
+                )
+
+        def regroup(on_vector, mat, h, g):
+            if ("gm", mat, h, g) not in t:
+                t["gm", mat, h, g] = keep.tile(
+                    [P, 4 * HALF], BF16, name="gm%d%d%d" % (mat, h, g), align_bytes=64
+                )
+            dst = t["gm", mat, h, g][:].rearrange("p (c i j) -> p c j i", i=4, j=4)
+            src = t["raw", mat, h][:, 4 * g : 4 * g + 4, :].rearrange("p j (c i) -> p c j i", i=4)
+            cv = NV[(mat, h)] // 4
+            if on_vector:
+                nc.vector.tensor_copy(out=dst[:, 0:cv], in_=src[:, 0:cv])
+            else:
+                nc.scalar.copy(out=dst[:, cv:], in_=src[:, cv:])
+
+        def quantise(key, label, width, src):
+            t[("c",) + key] = keep.tile([P, width], U32, name="c_" + label, align_bytes=64)
+            t[("s",) + key] = keep.tile([P, width], U8, name="s_" + label, align_bytes=64)
+            nc.vector.quantize_mx(out=t[("c",) + key][:].bitcast(FP8X4), scales=t[("s",) + key][:], in_=src)
+
+        def transpose_x(i):
+            xw = t["xp", i][:].bitcast(F32)
+            for mi in range(2):
+                tp = bank("tp")
+                t["tpx", i, mi] = tp
+                for j in range(4):
+                    lo = HALF * mi + 2 * P * (j // 2) + j % 2
+                    nc.tensor.transpose(tp[:, P * j : P * j + P], xw[:, lo : lo + 2 * P - 1 : 2], ident[:])
+
+        def copy_x(i, mi):
+            if ("gx", i) not in t:
+                t["gx", i] = keep.tile([P, 2 * D], BF16, name="gx%d" % i, align_bytes=64)
+            gw = t["gx", i][:].bitcast(F32)
+            nc.scalar.copy(
+                out=gw[:, HALF * mi : HALF * mi + HALF].rearrange("p (g b u) -> p g b u", g=2, u=2),
+                in_=t["tpx", i, mi][:].rearrange("p (g u b) -> p g b u", g=2, u=2),
+            )
+
+        def passes(stage_no, i, h):
+            for mi in range(2):
+                acc = bank("acc")
+                t["acc", stage_no, i, h, mi] = acc
+                for g in range(2):
+                    if stage_no == 1:
+                        key = ("x", i)
+                        lo = 256 * mi + P * g
+                    else:
+                        key = ("y", i, g)
+                        lo = P * mi
+                    nc.tensor.matmul_mx(
+                        out=acc[:],
+                        lhsT=t[("c",) + key][:, lo : lo + P].bitcast(FP8X4),
+                        lhsT_scale=t[("s",) + key][:, lo : lo + P],
+                        rhs=t["c", "m", stage_no - 1, h, g][:].bitcast(FP8X4),
+                        rhs_scale=t["s", "m", stage_no - 1, h, g][:],
+                        start=(g == 0),
+                        stop=(g == 1),
+                    )
+
+        def residual(stage_no, i, h):
+            for mi in range(2):
+                m = 2 * i + mi
+                if stage_no == 1:
+                    res = keep.tile([P, HALF], F32, name="x1_%d_%d" % (m, h))
+                    t["x1", m, h] = res
+                    old = t["xp", i][:, D * mi + HALF * h : D * mi + HALF * h + HALF]
+                else:
+                    res = stage.tile([P, HALF], F32, name="o", tag="o")
+                    old = t["x1", m, h][:]
+                acc = t["acc", stage_no, i, h, mi][:]
+                if stage_no == 1:
+                    acc = acc.rearrange("p (b j) -> p j b", j=4)
+                    old = old.rearrange("p (b j) -> p j b", j=4)
+                    new = res[:].rearrange("p (j b) -> p j b", j=4)
+                else:
+                    acc = acc.rearrange("p (b j) -> p b j", j=4)
+                    old = old.rearrange("p (j b) -> p b j", j=4)
+                    new = res[:].rearrange("p (b j) -> p b j", j=4)
+                nc.vector.scalar_tensor_tensor(
+                    out=new,
+                    in0=acc,
+                    scalar=c32[:, 2 * m + stage_no - 1 : 2 * m + stage_no],
+                    in1=old,
+                    op0=MULT,
+                    op1=ADD,
+                )
+                if stage_no == 2:
+                    nc.sync.dma_start(out=ov[:, m, HALF * h : HALF * h + HALF], in_=res[:])
+
+        def transpose_x1(i, h):
+            for mi in range(2):
+                tp = bank("tp")
+                t["tp1", i, h, mi] = tp
+                for j in range(4):
+                    nc.tensor.transpose(
+                        tp[:, P * j : P * j + P], t["x1", 2 * i + mi, h][:, P * j : P * j + P], ident[:]
+                    )
+
+        def copy_x1(i, h):
+            t["gx1", i, h] = keep.tile([P, D], BF16, name="gx1_%d_%d" % (i, h), align_bytes=64)
+            for mi in range(2):
+                nc.scalar.copy(
+                    out=t["gx1", i, h][:, HALF * mi : HALF * mi + HALF].rearrange("p (b j) -> p b j", j=4),
+                    in_=t["tp1", i, h, mi][:].rearrange("p (j b) -> p b j", j=4),
+                )
+
+        def fill_scalar(k):
+            for step in FILL_S.get(k, []):
+                if step[0] == "ex":
+                    copy_x(step[1], step[2])
+                else:
+                    regroup(False, step[1], step[2], step[3])
+
+        def fill_vector(k):
+            for step in FILL_V.get(k, []):
+                if step[0] == "rm":
+                    regroup(True, step[1], step[2], step[3])
+                elif step[0] == "qm":
+                    quantise(("m",) + step[1:], "m%d%d%d" % step[1:], HALF, t[("gm",) + step[1:]][:])
+                elif step[0] == "qx":
+                    quantise(("x", step[1]), "x%d" % step[1], HALF, t["gx", step[1]][:])
+                else:
+                    quantise(("y",) + step[1:], "y%d%d" % step[1:], 2 * P, t[("gx1",) + step[1:]][:])
+
+        for item in LOADS:
+            if item[0] == "x":
+                load_x(item[1])
+            else:
+                load_m(item[1], item[2])
+        for k in range(-1, len(GROUPS) + 1):
+            if 0 <= k < len(GROUPS):
+                passes(*GROUPS[k])
+            before = GROUPS[k - 1] if k >= 1 else (0, 0, 0)
+            if before[0] == 1:
+                transpose_x1(before[1], before[2])
+            for i in FILL_T.get(k, []):
+                transpose_x(i)
+            if before[0] == 1:
+                copy_x1(before[1], before[2])
+            fill_scalar(k)
+            if 0 <= k < len(GROUPS):
+                residual(*GROUPS[k])
+            fill_vector(k)

@@ -156,18 +156,9 @@ def tile_precomputedmetanet_pa_kernel(tc, transformed, coeff, task_mats, out):
                 else:
                     res = stage.tile([P, HALF], F32, name="o", tag="o")
                     old = t["x1", m, h][:]
-                acc = t["acc", stage_no, i, h, mi][:]
-                if stage_no == 1:
-                    acc = acc.rearrange("p (b j) -> p j b", j=4)
-                    old = old.rearrange("p (b j) -> p j b", j=4)
-                    new = res[:].rearrange("p (j b) -> p j b", j=4)
-                else:
-                    acc = acc.rearrange("p (b j) -> p b j", j=4)
-                    old = old.rearrange("p (j b) -> p b j", j=4)
-                    new = res[:].rearrange("p (b j) -> p b j", j=4)
                 nc.vector.scalar_tensor_tensor(
-                    out=new,
-                    in0=acc,
+                    out=res[:],
+                    in0=t["acc", stage_no, i, h, mi][:],
                     scalar=c32[:, 2 * m + stage_no - 1 : 2 * m + stage_no],
                     in1=old,
                     op0=MULT,
@@ -176,22 +167,32 @@ def tile_precomputedmetanet_pa_kernel(tc, transformed, coeff, task_mats, out):
                 if stage_no == 2:
                     nc.sync.dma_start(out=ov[:, m, HALF * h : HALF * h + HALF], in_=res[:])
 
-        def transpose_x1(i, h):
+        def round_x1(i, h):
+            xb = keep.tile([P, 2 * HALF], BF16, name="xb_%d_%d" % (i, h))
+            t["xb", i, h] = xb
             for mi in range(2):
-                tp = bank("tp")
-                t["tp1", i, h, mi] = tp
-                for j in range(4):
-                    nc.tensor.transpose(
-                        tp[:, P * j : P * j + P], t["x1", 2 * i + mi, h][:, P * j : P * j + P], ident[:]
-                    )
+                nc.gpsimd.tensor_scalar(
+                    out=xb[:, HALF * mi : HALF * mi + HALF].rearrange("p (u b e) -> p u b e", u=2, e=2),
+                    in0=t["x1", 2 * i + mi, h][:].rearrange("p (b u e) -> p u b e", u=2, e=2),
+                    scalar1=1.0,
+                    scalar2=0.0,
+                    op0=MULT,
+                    op1=ADD,
+                )
+
+        def transpose_x1(i, h):
+            tp = bank("tp")
+            t["tp1", i, h] = tp
+            xw = t["xb", i, h][:].bitcast(F32)
+            for j in range(4):
+                nc.tensor.transpose(tp[:, P * j : P * j + P], xw[:, P * j : P * j + P], ident[:])
 
         def copy_x1(i, h):
             t["gx1", i, h] = keep.tile([P, D], BF16, name="gx1_%d_%d" % (i, h), align_bytes=64)
-            for mi in range(2):
-                nc.scalar.copy(
-                    out=t["gx1", i, h][:, HALF * mi : HALF * mi + HALF].rearrange("p (b j) -> p b j", j=4),
-                    in_=t["tp1", i, h, mi][:].rearrange("p (j b) -> p b j", j=4),
-                )
+            nc.scalar.copy(
+                out=t["gx1", i, h][:].bitcast(F32).rearrange("p (m b u) -> p m b u", m=2, u=2),
+                in_=t["tp1", i, h][:].rearrange("p (m u b) -> p m b u", m=2, u=2),
+            )
 
         def fill_scalar(k):
             for step in FILL_S.get(k, []):
@@ -229,4 +230,6 @@ def tile_precomputedmetanet_pa_kernel(tc, transformed, coeff, task_mats, out):
             fill_scalar(k)
             if 0 <= k < len(GROUPS):
                 residual(*GROUPS[k])
+                if GROUPS[k][0] == 1:
+                    round_x1(GROUPS[k][1], GROUPS[k][2])
             fill_vector(k)

@@ -8,6 +8,7 @@ BF16 = mybir.dt.bfloat16
 U32 = mybir.dt.uint32
 U8 = mybir.dt.uint8
 FP8X4 = mybir.dt.float8_e4m3fn_x4
+COPY = mybir.ActivationFunctionType.Copy
 MULT = mybir.AluOpType.mult
 ADD = mybir.AluOpType.add
 
@@ -17,35 +18,8 @@ D = 1024
 HALF = 512
 FLOPS = 2 * 2 * 1024 * 1024 * 1024
 
-BANKS = 4
-NV = {(0, 0): 336, (0, 1): 320, (1, 0): 256, (1, 1): 0}
-LOADS = [("x", 0), ("m", 0, 0), ("x", 1), ("m", 0, 1), ("x", 2), ("x", 3), ("m", 1, 0), ("m", 1, 1)]
-GROUPS = [(1, 0, 0), (1, 1, 0), (1, 0, 1), (1, 1, 1), (1, 2, 0), (1, 2, 1), (2, 0, 0), (1, 3, 0), (2, 1, 0), (1, 3, 1), (2, 2, 0), (2, 0, 1), (2, 1, 1), (2, 2, 1), (2, 3, 0), (2, 3, 1)]
-FILL_T = {
-    -1: [0, 1],
-    1: [2],
-    2: [3],
-}
-FILL_S = {
-    -1: [("ex", 0, 0), ("rm", 0, 0, 0), ("ex", 0, 1), ("rm", 0, 0, 1), ("ex", 1, 0), ("rm", 0, 1, 0), ("ex", 1, 1), ("rm", 0, 1, 1)],
-    1: [("ex", 2, 0), ("ex", 2, 1), ("rm", 1, 0, 0)],
-    2: [("rm", 1, 0, 1), ("ex", 3, 0), ("ex", 3, 1)],
-    4: [("rm", 1, 1, 0)],
-    7: [("rm", 1, 1, 1)],
-}
-FILL_V = {
-    -1: [("rm", 0, 0, 0), ("qm", 0, 0, 0), ("rm", 0, 0, 1), ("qx", 0), ("qm", 0, 0, 1), ("rm", 0, 1, 0), ("qm", 0, 1, 0), ("qx", 1), ("rm", 0, 1, 1)],
-    0: [("qm", 0, 1, 1)],
-    1: [("q1", 0, 0)],
-    2: [("rm", 1, 0, 0), ("qx", 2), ("qm", 1, 0, 0)],
-    3: [("rm", 1, 0, 1)],
-    4: [("qx", 3), ("q1", 0, 1), ("qm", 1, 0, 1), ("q1", 1, 0), ("q1", 1, 1)],
-    6: [("qm", 1, 1, 0)],
-    8: [("q1", 2, 0), ("q1", 2, 1)],
-    9: [("qm", 1, 1, 1)],
-    10: [("q1", 3, 0)],
-    12: [("q1", 3, 1)],
-}
+BANKS = 8
+V_COLS = {(0, 0): 320, (0, 1): 320, (1, 0): 256, (1, 1): 192}
 
 
 def tile_precomputedmetanet_pa_kernel(tc, transformed, coeff, task_mats, out):
@@ -54,7 +28,7 @@ def tile_precomputedmetanet_pa_kernel(tc, transformed, coeff, task_mats, out):
     ov = out.rearrange("(p m) n -> p m n", m=NB)
     with ExitStack() as ctx:
         keep = ctx.enter_context(tc.tile_pool(name="keep", bufs=1))
-        stage = ctx.enter_context(tc.tile_pool(name="stage", bufs=8))
+        stage = ctx.enter_context(tc.tile_pool(name="stage", bufs=4))
         psum = ctx.enter_context(tc.psum_pool(name="psum", bufs=1))
         ctx.enter_context(tc.manual_schedule())
 
@@ -66,12 +40,12 @@ def tile_precomputedmetanet_pa_kernel(tc, transformed, coeff, task_mats, out):
         nc.vector.tensor_copy(out=c32[:], in_=c_bf[:])
 
         t = {}
-        count = {"tp": 0, "acc": 0}
+        used = []
 
-        def bank(kind):
-            k = count[kind]
-            count[kind] = k + 1
-            return psum.tile([P, HALF], F32, name="%s%d" % (kind, k % BANKS), tag="%s%d" % (kind, k % BANKS))
+        def bank():
+            k = len(used) % BANKS
+            used.append(k)
+            return psum.tile([P, HALF], F32, name="bank%d" % k, tag="bank%d" % k)
 
         def load_x(i):
             t["xp", i] = keep.tile([P, 2 * D], BF16, name="xp%d" % i)
@@ -79,55 +53,60 @@ def tile_precomputedmetanet_pa_kernel(tc, transformed, coeff, task_mats, out):
                 out=t["xp", i][:].rearrange("p (m k) -> p m k", m=2), in_=xv[:, 2 * i : 2 * i + 2, :]
             )
 
-        def load_m(mat, h):
-            raw = keep.tile([P, 8, HALF], BF16, name="raw%d_%d" % (mat, h))
-            t["raw", mat, h] = raw
-            cols = slice(HALF * h, HALF * h + HALF)
-            for g in range(2):
-                nc.sync.dma_start(
-                    out=raw[:, 4 * g : 4 * g + 4, :],
-                    in_=task_mats[mat, 512 * g : 512 * g + 512, cols].rearrange("(p j) c -> p j c", j=4),
-                )
+        def load_m(mat, h, g):
+            raw = keep.tile([P, 4, HALF], BF16, name="raw%d%d%d" % (mat, h, g))
+            t["raw", mat, h, g] = raw
+            nc.sync.dma_start(
+                out=raw[:],
+                in_=task_mats[mat, 512 * g : 512 * g + 512, HALF * h : HALF * h + HALF].rearrange(
+                    "(p j) c -> p j c", j=4
+                ),
+            )
 
-        def regroup(on_vector, mat, h, g):
+        def regroup(engine, mat, h, g, lo, hi):
             if ("gm", mat, h, g) not in t:
                 t["gm", mat, h, g] = keep.tile(
                     [P, 4 * HALF], BF16, name="gm%d%d%d" % (mat, h, g), align_bytes=64
                 )
-            dst = t["gm", mat, h, g][:].rearrange("p (c i j) -> p c j i", i=4, j=4)
-            src = t["raw", mat, h][:, 4 * g : 4 * g + 4, :].rearrange("p j (c i) -> p c j i", i=4)
-            cv = NV[(mat, h)] // 4
-            if on_vector:
-                nc.vector.tensor_copy(out=dst[:, 0:cv], in_=src[:, 0:cv])
+            dst = t["gm", mat, h, g][:].rearrange("p (c i j) -> p c j i", i=4, j=4)[:, lo // 4 : hi // 4]
+            src = t["raw", mat, h, g][:].rearrange("p j (c i) -> p c j i", i=4)[:, lo // 4 : hi // 4]
+            if engine == "v":
+                nc.vector.tensor_copy(out=dst, in_=src)
             else:
-                nc.scalar.copy(out=dst[:, cv:], in_=src[:, cv:])
+                nc.scalar.copy(out=dst, in_=src)
 
         def quantise(key, label, width, src):
             t[("c",) + key] = keep.tile([P, width], U32, name="c_" + label, align_bytes=64)
             t[("s",) + key] = keep.tile([P, width], U8, name="s_" + label, align_bytes=64)
             nc.vector.quantize_mx(out=t[("c",) + key][:].bitcast(FP8X4), scales=t[("s",) + key][:], in_=src)
 
-        def transpose_x(i):
+        def qm(mat, h, g):
+            quantise(("m", mat, h, g), "m%d%d%d" % (mat, h, g), HALF, t["gm", mat, h, g][:])
+
+        def tx(i):
             xw = t["xp", i][:].bitcast(F32)
             for mi in range(2):
-                tp = bank("tp")
+                tp = bank()
                 t["tpx", i, mi] = tp
                 for j in range(4):
                     lo = HALF * mi + 2 * P * (j // 2) + j % 2
                     nc.tensor.transpose(tp[:, P * j : P * j + P], xw[:, lo : lo + 2 * P - 1 : 2], ident[:])
 
-        def copy_x(i, mi):
-            if ("gx", i) not in t:
-                t["gx", i] = keep.tile([P, 2 * D], BF16, name="gx%d" % i, align_bytes=64)
+        def cx(i):
+            t["gx", i] = keep.tile([P, 2 * D], BF16, name="gx%d" % i, align_bytes=64)
             gw = t["gx", i][:].bitcast(F32)
-            nc.scalar.copy(
-                out=gw[:, HALF * mi : HALF * mi + HALF].rearrange("p (g b u) -> p g b u", g=2, u=2),
-                in_=t["tpx", i, mi][:].rearrange("p (g u b) -> p g b u", g=2, u=2),
-            )
-
-        def passes(stage_no, i, h):
             for mi in range(2):
-                acc = bank("acc")
+                nc.scalar.copy(
+                    out=gw[:, HALF * mi : HALF * mi + HALF].rearrange("p (g b u) -> p g b u", g=2, u=2),
+                    in_=t["tpx", i, mi][:].rearrange("p (g u b) -> p g b u", g=2, u=2),
+                )
+
+        def qx(i):
+            quantise(("x", i), "x%d" % i, HALF, t["gx", i][:])
+
+        def mx(stage_no, i, h):
+            for mi in range(2):
+                acc = bank()
                 t["acc", stage_no, i, h, mi] = acc
                 for g in range(2):
                     if stage_no == 1:
@@ -146,28 +125,21 @@ def tile_precomputedmetanet_pa_kernel(tc, transformed, coeff, task_mats, out):
                         stop=(g == 1),
                     )
 
-        def residual(stage_no, i, h):
+        def sum1(i, h):
             for mi in range(2):
                 m = 2 * i + mi
-                if stage_no == 1:
-                    res = keep.tile([P, HALF], F32, name="x1_%d_%d" % (m, h))
-                    t["x1", m, h] = res
-                    old = t["xp", i][:, D * mi + HALF * h : D * mi + HALF * h + HALF]
-                else:
-                    res = stage.tile([P, HALF], F32, name="o", tag="o")
-                    old = t["x1", m, h][:]
+                x1 = keep.tile([P, HALF], F32, name="x1_%d_%d" % (m, h))
+                t["x1", m, h] = x1
                 nc.vector.scalar_tensor_tensor(
-                    out=res[:],
-                    in0=t["acc", stage_no, i, h, mi][:],
-                    scalar=c32[:, 2 * m + stage_no - 1 : 2 * m + stage_no],
-                    in1=old,
+                    out=x1[:],
+                    in0=t["acc", 1, i, h, mi][:],
+                    scalar=c32[:, 2 * m : 2 * m + 1],
+                    in1=t["xp", i][:, D * mi + HALF * h : D * mi + HALF * h + HALF],
                     op0=MULT,
                     op1=ADD,
                 )
-                if stage_no == 2:
-                    nc.sync.dma_start(out=ov[:, m, HALF * h : HALF * h + HALF], in_=res[:])
 
-        def round_x1(i, h):
+        def round1(i, h):
             xb = keep.tile([P, 2 * HALF], BF16, name="xb_%d_%d" % (i, h))
             t["xb", i, h] = xb
             for mi in range(2):
@@ -180,56 +152,184 @@ def tile_precomputedmetanet_pa_kernel(tc, transformed, coeff, task_mats, out):
                     op1=ADD,
                 )
 
-        def transpose_x1(i, h):
-            tp = bank("tp")
+        def t1(i, h):
+            tp = bank()
             t["tp1", i, h] = tp
             xw = t["xb", i, h][:].bitcast(F32)
             for j in range(4):
                 nc.tensor.transpose(tp[:, P * j : P * j + P], xw[:, P * j : P * j + P], ident[:])
 
-        def copy_x1(i, h):
-            t["gx1", i, h] = keep.tile([P, D], BF16, name="gx1_%d_%d" % (i, h), align_bytes=64)
+        def c1(i, h):
+            gx = keep.tile([P, D], BF16, name="gx1_%d_%d" % (i, h), align_bytes=64)
+            t["gx1", i, h] = gx
             nc.scalar.copy(
-                out=t["gx1", i, h][:].bitcast(F32).rearrange("p (m b u) -> p m b u", m=2, u=2),
+                out=gx[:].bitcast(F32).rearrange("p (m b u) -> p m b u", m=2, u=2),
                 in_=t["tp1", i, h][:].rearrange("p (m u b) -> p m b u", m=2, u=2),
             )
 
-        def fill_scalar(k):
-            for step in FILL_S.get(k, []):
-                if step[0] == "ex":
-                    copy_x(step[1], step[2])
-                else:
-                    regroup(False, step[1], step[2], step[3])
+        def q1(i, h):
+            quantise(("y", i, h), "y%d%d" % (i, h), 2 * P, t["gx1", i, h][:])
 
-        def fill_vector(k):
-            for step in FILL_V.get(k, []):
-                if step[0] == "rm":
-                    regroup(True, step[1], step[2], step[3])
-                elif step[0] == "qm":
-                    quantise(("m",) + step[1:], "m%d%d%d" % step[1:], HALF, t[("gm",) + step[1:]][:])
-                elif step[0] == "qx":
-                    quantise(("x", step[1]), "x%d" % step[1], HALF, t["gx", step[1]][:])
+        def sum2(i, h, split):
+            for mi in range(2):
+                m = 2 * i + mi
+                acc = t["acc", 2, i, h, mi]
+                x1 = t["x1", m, h]
+                c = c32[:, 2 * m + 1 : 2 * m + 2]
+                if split and mi == 1:
+                    part = stage.tile([P, HALF], F32, name="part", tag="part")
+                    nc.scalar.activation(out=part[:], in_=acc[:], func=COPY, scale=c)
+                    nc.gpsimd.tensor_tensor(out=x1[:], in0=part[:], in1=x1[:], op=ADD)
                 else:
-                    quantise(("y",) + step[1:], "y%d%d" % step[1:], 2 * P, t[("gx1",) + step[1:]][:])
+                    nc.vector.scalar_tensor_tensor(
+                        out=x1[:], in0=acc[:], scalar=c, in1=x1[:], op0=MULT, op1=ADD
+                    )
 
-        for item in LOADS:
-            if item[0] == "x":
-                load_x(item[1])
-            else:
-                load_m(item[1], item[2])
-        for k in range(-1, len(GROUPS) + 1):
-            if 0 <= k < len(GROUPS):
-                passes(*GROUPS[k])
-            before = GROUPS[k - 1] if k >= 1 else (0, 0, 0)
-            if before[0] == 1:
-                transpose_x1(before[1], before[2])
-            for i in FILL_T.get(k, []):
-                transpose_x(i)
-            if before[0] == 1:
-                copy_x1(before[1], before[2])
-            fill_scalar(k)
-            if 0 <= k < len(GROUPS):
-                residual(*GROUPS[k])
-                if GROUPS[k][0] == 1:
-                    round_x1(GROUPS[k][1], GROUPS[k][2])
-            fill_vector(k)
+        def st(i, h, mi):
+            m = 2 * i + mi
+            nc.sync.dma_start(out=ov[:, m, HALF * h : HALF * h + HALF], in_=t["x1", m, h][:])
+
+        zeros = keep.tile([P, HALF], BF16, name="zeros")
+        nc.gpsimd.memset(zeros[:], 0.0)
+
+        def warm(n):
+            for k in range(n):
+                w = bank()
+                nc.tensor.matmul(w[:], zeros[:, 0:P], zeros[:], start=True, stop=True)
+
+        def rv(*k):
+            regroup("v", *k, 0, V_COLS[k[1:]])
+
+        def rs(*k):
+            regroup("s", *k, V_COLS[k[1:]], HALF)
+
+        def r1(h, g):
+            regroup("s", 1, h, g, 0, HALF)
+
+
+        load_x(0)
+        load_m(0, 0, 0)
+        load_m(0, 0, 1)
+        load_x(1)
+        load_m(0, 1, 0)
+        load_m(0, 1, 1)
+        load_x(2)
+        load_m(1, 0, 0)
+        load_x(3)
+        load_m(1, 0, 1)
+        load_m(1, 1, 0)
+        load_m(1, 1, 1)
+        warm(5)
+        tx(0)
+        cx(0)
+        warm(3)
+        rv(0, 0, 0)
+        rs(0, 0, 0)
+        rv(0, 0, 1)
+        qx(0)
+        qm(0, 0, 0)
+        rs(0, 0, 1)
+        tx(1)
+        cx(1)
+        rv(0, 1, 0)
+        qm(0, 0, 1)
+        mx(1, 0, 0)
+        qx(1)
+        mx(1, 1, 0)
+        rs(0, 1, 0)
+        rv(0, 1, 1)
+        rs(0, 1, 1)
+        qm(0, 1, 0)
+        sum1(0, 0)
+        round1(0, 0)
+        tx(2)
+        cx(2)
+        qm(0, 1, 1)
+        sum1(1, 0)
+        round1(1, 0)
+        mx(1, 0, 1)
+        mx(1, 1, 1)
+        r1(0, 0)
+        qx(2)
+        sum1(0, 1)
+        round1(0, 1)
+        t1(0, 0)
+        t1(1, 0)
+        tx(3)
+        c1(0, 0)
+        c1(1, 0)
+        cx(3)
+        sum1(1, 1)
+        round1(1, 1)
+        qm(1, 0, 0)
+        r1(0, 1)
+        mx(1, 2, 0)
+        mx(1, 2, 1)
+        q1(0, 0)
+        q1(1, 0)
+        sum1(2, 0)
+        round1(2, 0)
+        qx(3)
+        sum1(2, 1)
+        round1(2, 1)
+        t1(0, 1)
+        t1(1, 1)
+        c1(0, 1)
+        c1(1, 1)
+        mx(1, 3, 0)
+        mx(1, 3, 1)
+        r1(1, 0)
+        qm(1, 0, 1)
+        sum1(3, 0)
+        round1(3, 0)
+        q1(0, 1)
+        q1(1, 1)
+        sum1(3, 1)
+        round1(3, 1)
+        t1(2, 0)
+        t1(2, 1)
+        c1(2, 0)
+        c1(2, 1)
+        mx(2, 0, 0)
+        mx(2, 1, 0)
+        r1(1, 1)
+        qm(1, 1, 0)
+        q1(2, 0)
+        q1(2, 1)
+        sum2(0, 0, 1)
+        st(0, 0, 0)
+        t1(3, 0)
+        t1(3, 1)
+        c1(3, 0)
+        c1(3, 1)
+        qm(1, 1, 1)
+        sum2(1, 0, 1)
+        st(1, 0, 0)
+        mx(2, 2, 0)
+        mx(2, 0, 1)
+        q1(3, 0)
+        q1(3, 1)
+        sum2(2, 0, 1)
+        st(0, 0, 1)
+        st(2, 0, 0)
+        sum2(0, 1, 1)
+        st(0, 1, 0)
+        mx(2, 1, 1)
+        sum2(1, 1, 1)
+        st(1, 0, 1)
+        st(1, 1, 0)
+        mx(2, 2, 1)
+        sum2(2, 1, 0)
+        st(2, 1, 0)
+        st(2, 1, 1)
+        st(2, 0, 1)
+        mx(2, 3, 0)
+        sum2(3, 0, 0)
+        st(3, 0, 0)
+        st(0, 1, 1)
+        st(3, 0, 1)
+        mx(2, 3, 1)
+        sum2(3, 1, 0)
+        st(3, 1, 0)
+        st(1, 1, 1)
+        st(3, 1, 1)

@@ -8,7 +8,6 @@ BF16 = mybir.dt.bfloat16
 U32 = mybir.dt.uint32
 U8 = mybir.dt.uint8
 FP8X4 = mybir.dt.float8_e4m3fn_x4
-COPY = mybir.ActivationFunctionType.Copy
 MULT = mybir.AluOpType.mult
 ADD = mybir.AluOpType.add
 
@@ -19,7 +18,7 @@ HALF = 512
 FLOPS = 2 * 2 * 1024 * 1024 * 1024
 
 BANKS = 8
-V_COLS = {(0, 0): 320, (0, 1): 320, (1, 0): 256, (1, 1): 192}
+V_COLS = {(0, 0): 288, (0, 1): 256, (1, 0): 192, (1, 1): 192}
 
 
 def tile_precomputedmetanet_pa_kernel(tc, transformed, coeff, task_mats, out):
@@ -131,63 +130,53 @@ def tile_precomputedmetanet_pa_kernel(tc, transformed, coeff, task_mats, out):
                 x1 = keep.tile([P, HALF], F32, name="x1_%d_%d" % (m, h))
                 t["x1", m, h] = x1
                 nc.vector.scalar_tensor_tensor(
-                    out=x1[:],
-                    in0=t["acc", 1, i, h, mi][:],
+                    out=x1[:].rearrange("p (j b) -> p j b", j=4),
+                    in0=t["acc", 1, i, h, mi][:].rearrange("p (b j) -> p j b", j=4),
                     scalar=c32[:, 2 * m : 2 * m + 1],
-                    in1=t["xp", i][:, D * mi + HALF * h : D * mi + HALF * h + HALF],
-                    op0=MULT,
-                    op1=ADD,
-                )
-
-        def round1(i, h):
-            xb = keep.tile([P, 2 * HALF], BF16, name="xb_%d_%d" % (i, h))
-            t["xb", i, h] = xb
-            for mi in range(2):
-                nc.gpsimd.tensor_scalar(
-                    out=xb[:, HALF * mi : HALF * mi + HALF].rearrange("p (u b e) -> p u b e", u=2, e=2),
-                    in0=t["x1", 2 * i + mi, h][:].rearrange("p (b u e) -> p u b e", u=2, e=2),
-                    scalar1=1.0,
-                    scalar2=0.0,
+                    in1=t["xp", i][:, D * mi + HALF * h : D * mi + HALF * h + HALF].rearrange(
+                        "p (b j) -> p j b", j=4
+                    ),
                     op0=MULT,
                     op1=ADD,
                 )
 
         def t1(i, h):
-            tp = bank()
-            t["tp1", i, h] = tp
-            xw = t["xb", i, h][:].bitcast(F32)
-            for j in range(4):
-                nc.tensor.transpose(tp[:, P * j : P * j + P], xw[:, P * j : P * j + P], ident[:])
+            for mi in range(2):
+                tp = bank()
+                t["tp1", i, h, mi] = tp
+                for j in range(4):
+                    nc.tensor.transpose(
+                        tp[:, P * j : P * j + P], t["x1", 2 * i + mi, h][:, P * j : P * j + P], ident[:]
+                    )
 
         def c1(i, h):
             gx = keep.tile([P, D], BF16, name="gx1_%d_%d" % (i, h), align_bytes=64)
             t["gx1", i, h] = gx
-            nc.scalar.copy(
-                out=gx[:].bitcast(F32).rearrange("p (m b u) -> p m b u", m=2, u=2),
-                in_=t["tp1", i, h][:].rearrange("p (m u b) -> p m b u", m=2, u=2),
-            )
+            for mi in range(2):
+                nc.scalar.copy(
+                    out=gx[:, HALF * mi : HALF * mi + HALF].rearrange("p (b j) -> p b j", j=4),
+                    in_=t["tp1", i, h, mi][:].rearrange("p (j b) -> p b j", j=4),
+                )
 
         def q1(i, h):
             quantise(("y", i, h), "y%d%d" % (i, h), 2 * P, t["gx1", i, h][:])
 
-        def sum2(i, h, split):
+        def sum2(i, h):
             for mi in range(2):
                 m = 2 * i + mi
                 acc = t["acc", 2, i, h, mi]
-                x1 = t["x1", m, h]
                 c = c32[:, 2 * m + 1 : 2 * m + 2]
-                if split and mi == 1:
-                    part = stage.tile([P, HALF], F32, name="part", tag="part")
-                    nc.scalar.activation(out=part[:], in_=acc[:], func=COPY, scale=c)
-                    nc.gpsimd.tensor_tensor(out=x1[:], in0=part[:], in1=x1[:], op=ADD)
-                else:
-                    nc.vector.scalar_tensor_tensor(
-                        out=x1[:], in0=acc[:], scalar=c, in1=x1[:], op0=MULT, op1=ADD
-                    )
+                res = stage.tile([P, HALF], F32, name="o", tag="o", bufs=12)
+                t["res", m, h] = res
+                new = res[:].rearrange("p (b j) -> p b j", j=4)
+                old = t["x1", m, h][:].rearrange("p (j b) -> p b j", j=4)
+                nc.vector.scalar_tensor_tensor(
+                    out=new, in0=acc[:].rearrange("p (b j) -> p b j", j=4), scalar=c, in1=old, op0=MULT, op1=ADD
+                )
 
         def st(i, h, mi):
             m = 2 * i + mi
-            nc.sync.dma_start(out=ov[:, m, HALF * h : HALF * h + HALF], in_=t["x1", m, h][:])
+            nc.sync.dma_start(out=ov[:, m, HALF * h : HALF * h + HALF], in_=t["res", m, h][:])
 
         zeros = keep.tile([P, HALF], BF16, name="zeros")
         nc.gpsimd.memset(zeros[:], 0.0)
@@ -209,69 +198,64 @@ def tile_precomputedmetanet_pa_kernel(tc, transformed, coeff, task_mats, out):
 
         load_x(0)
         load_m(0, 0, 0)
-        load_m(0, 0, 1)
         load_x(1)
-        load_m(0, 1, 0)
-        load_m(0, 1, 1)
+        load_m(0, 0, 1)
         load_x(2)
-        load_m(1, 0, 0)
+        load_m(0, 1, 0)
         load_x(3)
+        load_m(0, 1, 1)
+        load_m(1, 0, 0)
         load_m(1, 0, 1)
         load_m(1, 1, 0)
         load_m(1, 1, 1)
-        warm(5)
+        warm(6)
         tx(0)
         cx(0)
-        warm(3)
+        warm(2)
         rv(0, 0, 0)
         rs(0, 0, 0)
-        rv(0, 0, 1)
         qx(0)
-        qm(0, 0, 0)
-        rs(0, 0, 1)
         tx(1)
         cx(1)
-        rv(0, 1, 0)
-        qm(0, 0, 1)
-        mx(1, 0, 0)
+        warm(3)
+        rv(0, 0, 1)
+        rs(0, 0, 1)
+        qm(0, 0, 0)
         qx(1)
-        mx(1, 1, 0)
-        rs(0, 1, 0)
-        rv(0, 1, 1)
-        rs(0, 1, 1)
-        qm(0, 1, 0)
-        sum1(0, 0)
-        round1(0, 0)
+        qm(0, 0, 1)
         tx(2)
         cx(2)
+        mx(1, 0, 0)
+        mx(1, 1, 0)
+        rv(0, 1, 0)
+        rs(0, 1, 0)
+        tx(3)
+        sum1(0, 0)
+        rv(0, 1, 1)
+        rs(0, 1, 1)
+        cx(3)
+        qm(0, 1, 0)
         qm(0, 1, 1)
         sum1(1, 0)
-        round1(1, 0)
+        qx(2)
         mx(1, 0, 1)
         mx(1, 1, 1)
+        qx(3)
         r1(0, 0)
-        qx(2)
         sum1(0, 1)
-        round1(0, 1)
         t1(0, 0)
         t1(1, 0)
-        tx(3)
         c1(0, 0)
         c1(1, 0)
-        cx(3)
         sum1(1, 1)
-        round1(1, 1)
-        qm(1, 0, 0)
-        r1(0, 1)
         mx(1, 2, 0)
         mx(1, 2, 1)
+        r1(0, 1)
+        qm(1, 0, 0)
         q1(0, 0)
-        q1(1, 0)
         sum1(2, 0)
-        round1(2, 0)
-        qx(3)
+        q1(1, 0)
         sum1(2, 1)
-        round1(2, 1)
         t1(0, 1)
         t1(1, 1)
         c1(0, 1)
@@ -281,11 +265,9 @@ def tile_precomputedmetanet_pa_kernel(tc, transformed, coeff, task_mats, out):
         r1(1, 0)
         qm(1, 0, 1)
         sum1(3, 0)
-        round1(3, 0)
         q1(0, 1)
         q1(1, 1)
         sum1(3, 1)
-        round1(3, 1)
         t1(2, 0)
         t1(2, 1)
         c1(2, 0)
@@ -294,42 +276,42 @@ def tile_precomputedmetanet_pa_kernel(tc, transformed, coeff, task_mats, out):
         mx(2, 1, 0)
         r1(1, 1)
         qm(1, 1, 0)
+        sum2(0, 0)
+        st(0, 0, 0)
+        st(0, 0, 1)
         q1(2, 0)
         q1(2, 1)
-        sum2(0, 0, 1)
-        st(0, 0, 0)
         t1(3, 0)
         t1(3, 1)
         c1(3, 0)
         c1(3, 1)
-        qm(1, 1, 1)
-        sum2(1, 0, 1)
+        sum2(1, 0)
         st(1, 0, 0)
+        st(1, 0, 1)
+        qm(1, 1, 1)
         mx(2, 2, 0)
         mx(2, 0, 1)
+        sum2(2, 0)
+        st(2, 0, 0)
+        st(2, 0, 1)
         q1(3, 0)
         q1(3, 1)
-        sum2(2, 0, 1)
-        st(0, 0, 1)
-        st(2, 0, 0)
-        sum2(0, 1, 1)
+        sum2(0, 1)
         st(0, 1, 0)
+        st(0, 1, 1)
         mx(2, 1, 1)
-        sum2(1, 1, 1)
-        st(1, 0, 1)
+        sum2(1, 1)
         st(1, 1, 0)
+        st(1, 1, 1)
         mx(2, 2, 1)
-        sum2(2, 1, 0)
+        sum2(2, 1)
         st(2, 1, 0)
         st(2, 1, 1)
-        st(2, 0, 1)
         mx(2, 3, 0)
-        sum2(3, 0, 0)
+        sum2(3, 0)
         st(3, 0, 0)
-        st(0, 1, 1)
         st(3, 0, 1)
         mx(2, 3, 1)
-        sum2(3, 1, 0)
+        sum2(3, 1)
         st(3, 1, 0)
-        st(1, 1, 1)
         st(3, 1, 1)

@@ -18,7 +18,7 @@ HALF = 512
 FLOPS = 2 * 2 * 1024 * 1024 * 1024
 
 BANKS = 8
-V_COLS = {(0, 0): 288, (0, 1): 256, (1, 0): 192, (1, 1): 192}
+V_COLS = {(0, 0, 0): 320, (0, 0, 1): 320, (0, 1, 0): 256, (0, 1, 1): 256, (1, 0, 0): 128, (1, 0, 1): 128, (1, 1, 0): 128, (1, 1, 1): 192}
 
 
 def tile_precomputedmetanet_pa_kernel(tc, transformed, coeff, task_mats, out):
@@ -166,7 +166,7 @@ def tile_precomputedmetanet_pa_kernel(tc, transformed, coeff, task_mats, out):
                 m = 2 * i + mi
                 acc = t["acc", 2, i, h, mi]
                 c = c32[:, 2 * m + 1 : 2 * m + 2]
-                res = stage.tile([P, HALF], F32, name="o", tag="o", bufs=12)
+                res = stage.tile([P, HALF], F32, name="o", tag="o", bufs=8)
                 t["res", m, h] = res
                 new = res[:].rearrange("p (b j) -> p b j", j=4)
                 old = t["x1", m, h][:].rearrange("p (j b) -> p b j", j=4)
@@ -187,13 +187,10 @@ def tile_precomputedmetanet_pa_kernel(tc, transformed, coeff, task_mats, out):
                 nc.tensor.matmul(w[:], zeros[:, 0:P], zeros[:], start=True, stop=True)
 
         def rv(*k):
-            regroup("v", *k, 0, V_COLS[k[1:]])
+            regroup("v", *k, 0, V_COLS[k])
 
         def rs(*k):
-            regroup("s", *k, V_COLS[k[1:]], HALF)
-
-        def r1(h, g):
-            regroup("s", 1, h, g, 0, HALF)
+            regroup("s", *k, V_COLS[k], HALF)
 
 
         load_x(0)
@@ -217,7 +214,7 @@ def tile_precomputedmetanet_pa_kernel(tc, transformed, coeff, task_mats, out):
         qx(0)
         tx(1)
         cx(1)
-        warm(3)
+        warm(2)
         rv(0, 0, 1)
         rs(0, 0, 1)
         qm(0, 0, 0)
@@ -241,31 +238,34 @@ def tile_precomputedmetanet_pa_kernel(tc, transformed, coeff, task_mats, out):
         mx(1, 0, 1)
         mx(1, 1, 1)
         qx(3)
-        r1(0, 0)
+        rs(1, 0, 0)
         sum1(0, 1)
         t1(0, 0)
         t1(1, 0)
         c1(0, 0)
         c1(1, 0)
         sum1(1, 1)
+        rv(1, 0, 0)
         mx(1, 2, 0)
         mx(1, 2, 1)
-        r1(0, 1)
-        qm(1, 0, 0)
+        rs(1, 0, 1)
         q1(0, 0)
         sum1(2, 0)
         q1(1, 0)
+        qm(1, 0, 0)
         sum1(2, 1)
+        rv(1, 0, 1)
         t1(0, 1)
         t1(1, 1)
         c1(0, 1)
         c1(1, 1)
         mx(1, 3, 0)
         mx(1, 3, 1)
-        r1(1, 0)
-        qm(1, 0, 1)
+        rs(1, 1, 0)
+        rv(1, 1, 0)
         sum1(3, 0)
         q1(0, 1)
+        qm(1, 0, 1)
         q1(1, 1)
         sum1(3, 1)
         t1(2, 0)
@@ -274,7 +274,8 @@ def tile_precomputedmetanet_pa_kernel(tc, transformed, coeff, task_mats, out):
         c1(2, 1)
         mx(2, 0, 0)
         mx(2, 1, 0)
-        r1(1, 1)
+        rv(1, 1, 1)
+        rs(1, 1, 1)
         qm(1, 1, 0)
         sum2(0, 0)
         st(0, 0, 0)
@@ -291,11 +292,11 @@ def tile_precomputedmetanet_pa_kernel(tc, transformed, coeff, task_mats, out):
         qm(1, 1, 1)
         mx(2, 2, 0)
         mx(2, 0, 1)
+        q1(3, 0)
+        q1(3, 1)
         sum2(2, 0)
         st(2, 0, 0)
         st(2, 0, 1)
-        q1(3, 0)
-        q1(3, 1)
         sum2(0, 1)
         st(0, 1, 0)
         st(0, 1, 1)

@@ -18,7 +18,6 @@ HALF = 512
 FLOPS = 2 * 2 * 1024 * 1024 * 1024
 
 BANKS = 8
-V_COLS = {(0, 0, 0): 320, (0, 0, 1): 320, (0, 1, 0): 256, (0, 1, 1): 256, (1, 0, 0): 128, (1, 0, 1): 128, (1, 1, 0): 128, (1, 1, 1): 192}
 
 
 def tile_precomputedmetanet_pa_kernel(tc, transformed, coeff, task_mats, out):
@@ -35,8 +34,6 @@ def tile_precomputedmetanet_pa_kernel(tc, transformed, coeff, task_mats, out):
         make_identity(nc, ident[:])
         c_bf = keep.tile([P, 2 * NB], BF16, name="c_bf")
         nc.scalar.dma_start(out=c_bf[:], in_=coeff.rearrange("(p m) j -> p (m j)", m=NB))
-        c32 = keep.tile([P, 2 * NB], F32, name="c32")
-        nc.vector.tensor_copy(out=c32[:], in_=c_bf[:])
 
         t = {}
         used = []
@@ -52,23 +49,30 @@ def tile_precomputedmetanet_pa_kernel(tc, transformed, coeff, task_mats, out):
                 out=t["xp", i][:].rearrange("p (m k) -> p m k", m=2), in_=xv[:, 2 * i : 2 * i + 2, :]
             )
 
-        def load_m(mat, h, g):
-            raw = keep.tile([P, 4, HALF], BF16, name="raw%d%d%d" % (mat, h, g))
-            t["raw", mat, h, g] = raw
+        def load_m0(h, g):
+            raw = keep.tile([P, 4, HALF], BF16, name="raw0%d%d" % (h, g))
+            t["raw", 0, h, g] = raw[:]
             nc.sync.dma_start(
                 out=raw[:],
-                in_=task_mats[mat, 512 * g : 512 * g + 512, HALF * h : HALF * h + HALF].rearrange(
+                in_=task_mats[0, 512 * g : 512 * g + 512, HALF * h : HALF * h + HALF].rearrange(
                     "(p j) c -> p j c", j=4
                 ),
             )
 
-        def regroup(engine, mat, h, g, lo, hi):
-            if ("gm", mat, h, g) not in t:
-                t["gm", mat, h, g] = keep.tile(
-                    [P, 4 * HALF], BF16, name="gm%d%d%d" % (mat, h, g), align_bytes=64
-                )
-            dst = t["gm", mat, h, g][:].rearrange("p (c i j) -> p c j i", i=4, j=4)[:, lo // 4 : hi // 4]
-            src = t["raw", mat, h, g][:].rearrange("p j (c i) -> p c j i", i=4)[:, lo // 4 : hi // 4]
+        def load_m1(g):
+            raw = keep.tile([P, 4, D], BF16, name="raw1%d" % g)
+            for h in range(2):
+                t["raw", 1, h, g] = raw[:, :, HALF * h : HALF * h + HALF]
+            nc.sync.dma_start(
+                out=raw[:], in_=task_mats[1, 512 * g : 512 * g + 512, :].rearrange("(p j) c -> p j c", j=4)
+            )
+
+        def regroup(engine, mat, h, g, lo=0, hi=HALF):
+            if ("gm", mat, h) not in t:
+                t["gm", mat, h] = keep.tile([P, 8 * HALF], BF16, name="gm%d%d" % (mat, h), align_bytes=64)
+            gm = t["gm", mat, h][:, 4 * HALF * g : 4 * HALF * g + 4 * HALF]
+            dst = gm.rearrange("p (c i j) -> p c j i", i=4, j=4)[:, lo // 4 : hi // 4]
+            src = t["raw", mat, h, g].rearrange("p j (c i) -> p c j i", i=4)[:, lo // 4 : hi // 4]
             if engine == "v":
                 nc.vector.tensor_copy(out=dst, in_=src)
             else:
@@ -79,8 +83,14 @@ def tile_precomputedmetanet_pa_kernel(tc, transformed, coeff, task_mats, out):
             t[("s",) + key] = keep.tile([P, width], U8, name="s_" + label, align_bytes=64)
             nc.vector.quantize_mx(out=t[("c",) + key][:].bitcast(FP8X4), scales=t[("s",) + key][:], in_=src)
 
-        def qm(mat, h, g):
-            quantise(("m", mat, h, g), "m%d%d%d" % (mat, h, g), HALF, t["gm", mat, h, g][:])
+        def qm(mat, h, *gs):
+            width = HALF * len(gs)
+            lo = 4 * HALF * gs[0]
+            key = ("m", mat, h, gs)
+            quantise(key, "m%d%d%d" % (mat, h, gs[0]), width, t["gm", mat, h][:, lo : lo + 4 * width])
+            for n, g in enumerate(gs):
+                for kind in ("c", "s"):
+                    t[kind, "m", mat, h, g] = t[(kind,) + key][:, HALF * n : HALF * n + HALF]
 
         def tx(i):
             xw = t["xp", i][:].bitcast(F32)
@@ -112,14 +122,14 @@ def tile_precomputedmetanet_pa_kernel(tc, transformed, coeff, task_mats, out):
                         key = ("x", i)
                         lo = 256 * mi + P * g
                     else:
-                        key = ("y", i, g)
-                        lo = P * mi
+                        key = ("y", i)
+                        lo = 2 * P * g + P * mi
                     nc.tensor.matmul_mx(
                         out=acc[:],
                         lhsT=t[("c",) + key][:, lo : lo + P].bitcast(FP8X4),
                         lhsT_scale=t[("s",) + key][:, lo : lo + P],
-                        rhs=t["c", "m", stage_no - 1, h, g][:].bitcast(FP8X4),
-                        rhs_scale=t["s", "m", stage_no - 1, h, g][:],
+                        rhs=t["c", "m", stage_no - 1, h, g].bitcast(FP8X4),
+                        rhs_scale=t["s", "m", stage_no - 1, h, g],
                         start=(g == 0),
                         stop=(g == 1),
                     )
@@ -132,7 +142,7 @@ def tile_precomputedmetanet_pa_kernel(tc, transformed, coeff, task_mats, out):
                 nc.vector.scalar_tensor_tensor(
                     out=x1[:].rearrange("p (j b) -> p j b", j=4),
                     in0=t["acc", 1, i, h, mi][:].rearrange("p (b j) -> p j b", j=4),
-                    scalar=c32[:, 2 * m : 2 * m + 1],
+                    scalar=c_bf[:, 2 * m : 2 * m + 1],
                     in1=t["xp", i][:, D * mi + HALF * h : D * mi + HALF * h + HALF].rearrange(
                         "p (b j) -> p j b", j=4
                     ),
@@ -150,23 +160,24 @@ def tile_precomputedmetanet_pa_kernel(tc, transformed, coeff, task_mats, out):
                     )
 
         def c1(i, h):
-            gx = keep.tile([P, D], BF16, name="gx1_%d_%d" % (i, h), align_bytes=64)
-            t["gx1", i, h] = gx
+            if h == 0:
+                t["gx1", i] = keep.tile([P, 2 * D], BF16, name="gx1_%d" % i, align_bytes=64)
+            gx = t["gx1", i][:, D * h : D * h + D]
             for mi in range(2):
                 nc.scalar.copy(
                     out=gx[:, HALF * mi : HALF * mi + HALF].rearrange("p (b j) -> p b j", j=4),
                     in_=t["tp1", i, h, mi][:].rearrange("p (j b) -> p b j", j=4),
                 )
 
-        def q1(i, h):
-            quantise(("y", i, h), "y%d%d" % (i, h), 2 * P, t["gx1", i, h][:])
+        def q1(i):
+            quantise(("y", i), "y%d" % i, 4 * P, t["gx1", i][:])
 
         def sum2(i, h):
             for mi in range(2):
                 m = 2 * i + mi
                 acc = t["acc", 2, i, h, mi]
-                c = c32[:, 2 * m + 1 : 2 * m + 2]
-                res = stage.tile([P, HALF], F32, name="o", tag="o", bufs=8)
+                c = c_bf[:, 2 * m + 1 : 2 * m + 2]
+                res = stage.tile([P, HALF], F32, name="o", tag="o", bufs=16)
                 t["res", m, h] = res
                 new = res[:].rearrange("p (b j) -> p b j", j=4)
                 old = t["x1", m, h][:].rearrange("p (j b) -> p b j", j=4)
@@ -187,57 +198,49 @@ def tile_precomputedmetanet_pa_kernel(tc, transformed, coeff, task_mats, out):
                 nc.tensor.matmul(w[:], zeros[:, 0:P], zeros[:], start=True, stop=True)
 
         def rv(*k):
-            regroup("v", *k, 0, V_COLS[k])
+            regroup("v", *k)
 
         def rs(*k):
-            regroup("s", *k, V_COLS[k], HALF)
+            regroup("s", *k)
 
 
+        load_m0(0, 0)
         load_x(0)
-        load_m(0, 0, 0)
+        load_m0(0, 1)
         load_x(1)
-        load_m(0, 0, 1)
+        load_m0(1, 0)
         load_x(2)
-        load_m(0, 1, 0)
+        load_m0(1, 1)
         load_x(3)
-        load_m(0, 1, 1)
-        load_m(1, 0, 0)
-        load_m(1, 0, 1)
-        load_m(1, 1, 0)
-        load_m(1, 1, 1)
+        load_m1(0)
+        load_m1(1)
         warm(6)
         tx(0)
         cx(0)
         warm(2)
         rv(0, 0, 0)
-        rs(0, 0, 0)
+        qm(0, 0, 0)
+        rv(0, 0, 1)
         qx(0)
+        qm(0, 0, 1)
         tx(1)
         cx(1)
-        warm(2)
-        rv(0, 0, 1)
-        rs(0, 0, 1)
-        qm(0, 0, 0)
-        qx(1)
-        qm(0, 0, 1)
-        tx(2)
-        cx(2)
         mx(1, 0, 0)
-        mx(1, 1, 0)
-        rv(0, 1, 0)
         rs(0, 1, 0)
-        tx(3)
+        qx(1)
+        tx(2)
+        mx(1, 1, 0)
         sum1(0, 0)
         rv(0, 1, 1)
-        rs(0, 1, 1)
+        cx(2)
+        tx(3)
         cx(3)
         qm(0, 1, 0)
         qm(0, 1, 1)
         sum1(1, 0)
-        qx(2)
         mx(1, 0, 1)
         mx(1, 1, 1)
-        qx(3)
+        qx(2)
         rs(1, 0, 0)
         sum1(0, 1)
         t1(0, 0)
@@ -245,58 +248,50 @@ def tile_precomputedmetanet_pa_kernel(tc, transformed, coeff, task_mats, out):
         c1(0, 0)
         c1(1, 0)
         sum1(1, 1)
-        rv(1, 0, 0)
+        qx(3)
         mx(1, 2, 0)
         mx(1, 2, 1)
         rs(1, 0, 1)
-        q1(0, 0)
         sum1(2, 0)
-        q1(1, 0)
-        qm(1, 0, 0)
-        sum1(2, 1)
-        rv(1, 0, 1)
         t1(0, 1)
         t1(1, 1)
         c1(0, 1)
         c1(1, 1)
+        sum1(2, 1)
         mx(1, 3, 0)
         mx(1, 3, 1)
-        rs(1, 1, 0)
-        rv(1, 1, 0)
+        rv(1, 1, 1, 0, 192)
         sum1(3, 0)
-        q1(0, 1)
-        qm(1, 0, 1)
-        q1(1, 1)
+        qm(1, 0, 0, 1)
+        q1(0)
+        q1(1)
         sum1(3, 1)
+        rs(1, 1, 0)
         t1(2, 0)
         t1(2, 1)
         c1(2, 0)
         c1(2, 1)
+        rs(1, 1, 1, 192, 512)
         mx(2, 0, 0)
         mx(2, 1, 0)
-        rv(1, 1, 1)
-        rs(1, 1, 1)
-        qm(1, 1, 0)
         sum2(0, 0)
         st(0, 0, 0)
         st(0, 0, 1)
-        q1(2, 0)
-        q1(2, 1)
         t1(3, 0)
         t1(3, 1)
         c1(3, 0)
         c1(3, 1)
+        q1(2)
         sum2(1, 0)
         st(1, 0, 0)
         st(1, 0, 1)
-        qm(1, 1, 1)
         mx(2, 2, 0)
+        qm(1, 1, 0, 1)
         mx(2, 0, 1)
-        q1(3, 0)
-        q1(3, 1)
         sum2(2, 0)
         st(2, 0, 0)
         st(2, 0, 1)
+        q1(3)
         sum2(0, 1)
         st(0, 1, 0)
         st(0, 1, 1)

@@ -75,6 +75,15 @@ def tile_precomputedmetanet_pa_kernel(tc, transformed, coeff, task_mats, out):
             src = t["raw", mat, h, g].rearrange("p j (c i) -> p c j i", i=4)[:, lo // 4 : hi // 4]
             if engine == "v":
                 nc.vector.tensor_copy(out=dst, in_=src)
+            elif engine == "g":
+                nc.gpsimd.tensor_scalar(
+                    out=gm[:, 4 * lo : 4 * hi].rearrange("p (c j) -> p c j", j=4),
+                    in0=t["raw", mat, h, g][:, :, lo:hi].rearrange("p j c -> p c j"),
+                    scalar1=1.0,
+                    scalar2=0.0,
+                    op0=MULT,
+                    op1=ADD,
+                )
             else:
                 nc.scalar.copy(out=dst, in_=src)
 
@@ -200,6 +209,10 @@ def tile_precomputedmetanet_pa_kernel(tc, transformed, coeff, task_mats, out):
         def rv(*k):
             regroup("v", *k)
 
+        def rg(mat, h, g):
+            for lo in range(0, HALF, P):
+                regroup("g", mat, h, g, lo, lo + P)
+
         def rs(*k):
             regroup("s", *k)
 
@@ -241,6 +254,7 @@ def tile_precomputedmetanet_pa_kernel(tc, transformed, coeff, task_mats, out):
         mx(1, 0, 1)
         mx(1, 1, 1)
         qx(2)
+        rg(1, 0, 1)
         rs(1, 0, 0)
         sum1(0, 1)
         t1(0, 0)
@@ -251,7 +265,7 @@ def tile_precomputedmetanet_pa_kernel(tc, transformed, coeff, task_mats, out):
         qx(3)
         mx(1, 2, 0)
         mx(1, 2, 1)
-        rs(1, 0, 1)
+        rs(1, 1, 0)
         sum1(2, 0)
         t1(0, 1)
         t1(1, 1)
@@ -260,38 +274,31 @@ def tile_precomputedmetanet_pa_kernel(tc, transformed, coeff, task_mats, out):
         sum1(2, 1)
         mx(1, 3, 0)
         mx(1, 3, 1)
-        rv(1, 1, 1, 0, 192)
-        sum1(3, 0)
         qm(1, 0, 0, 1)
+        sum1(3, 0)
         q1(0)
         q1(1)
         sum1(3, 1)
-        rs(1, 1, 0)
+        rs(1, 1, 1)
         t1(2, 0)
         t1(2, 1)
         c1(2, 0)
         c1(2, 1)
-        rs(1, 1, 1, 192, 512)
         mx(2, 0, 0)
         mx(2, 1, 0)
         sum2(0, 0)
         st(0, 0, 0)
         st(0, 0, 1)
+        qm(1, 1, 0, 1)
         t1(3, 0)
         t1(3, 1)
         c1(3, 0)
         c1(3, 1)
-        q1(2)
         sum2(1, 0)
         st(1, 0, 0)
         st(1, 0, 1)
-        mx(2, 2, 0)
-        qm(1, 1, 0, 1)
         mx(2, 0, 1)
-        sum2(2, 0)
-        st(2, 0, 0)
-        st(2, 0, 1)
-        q1(3)
+        q1(2)
         sum2(0, 1)
         st(0, 1, 0)
         st(0, 1, 1)
@@ -299,6 +306,11 @@ def tile_precomputedmetanet_pa_kernel(tc, transformed, coeff, task_mats, out):
         sum2(1, 1)
         st(1, 1, 0)
         st(1, 1, 1)
+        q1(3)
+        mx(2, 2, 0)
+        sum2(2, 0)
+        st(2, 0, 0)
+        st(2, 0, 1)
         mx(2, 2, 1)
         sum2(2, 1)
         st(2, 1, 0)

from contextlib import ExitStack

import concourse.mybir as mybir
from concourse.masks import make_identity

F32 = mybir.dt.float32
BF16 = mybir.dt.bfloat16
U32 = mybir.dt.uint32
U8 = mybir.dt.uint8
FP8X4 = mybir.dt.float8_e4m3fn_x4
MULT = mybir.AluOpType.mult
ADD = mybir.AluOpType.add

P = 128
NB = 8
D = 1024
HALF = 512
FLOPS = 2 * 2 * 1024 * 1024 * 1024

BANKS = 8


def tile_precomputedmetanet_pa_kernel(tc, transformed, coeff, task_mats, out):
    nc = tc.nc
    xv = transformed.rearrange("(p m) k -> p m k", m=NB)
    ov = out.rearrange("(p m) n -> p m n", m=NB)
    with ExitStack() as ctx:
        keep = ctx.enter_context(tc.tile_pool(name="keep", bufs=1))
        stage = ctx.enter_context(tc.tile_pool(name="stage", bufs=4))
        psum = ctx.enter_context(tc.psum_pool(name="psum", bufs=1))
        ctx.enter_context(tc.manual_schedule())

        ident = keep.tile([P, P], F32, name="ident")
        make_identity(nc, ident[:])
        c_bf = keep.tile([P, 2 * NB], BF16, name="c_bf")
        nc.scalar.dma_start(out=c_bf[:], in_=coeff.rearrange("(p m) j -> p (m j)", m=NB))

        t = {}
        used = []

        def bank():
            k = len(used) % BANKS
            used.append(k)
            return psum.tile([P, HALF], F32, name="bank%d" % k, tag="bank%d" % k)

        def load_x(i):
            t["xp", i] = keep.tile([P, 2 * D], BF16, name="xp%d" % i)
            nc.sync.dma_start(
                out=t["xp", i][:].rearrange("p (m k) -> p m k", m=2), in_=xv[:, 2 * i : 2 * i + 2, :]
            )

        def load_m0(h, g):
            raw = keep.tile([P, 4, HALF], BF16, name="raw0%d%d" % (h, g))
            t["raw", 0, h, g] = raw[:]
            nc.sync.dma_start(
                out=raw[:],
                in_=task_mats[0, 512 * g : 512 * g + 512, HALF * h : HALF * h + HALF].rearrange(
                    "(p j) c -> p j c", j=4
                ),
            )

        def load_m1(g):
            raw = keep.tile([P, 4, D], BF16, name="raw1%d" % g)
            for h in range(2):
                t["raw", 1, h, g] = raw[:, :, HALF * h : HALF * h + HALF]
            nc.sync.dma_start(
                out=raw[:], in_=task_mats[1, 512 * g : 512 * g + 512, :].rearrange("(p j) c -> p j c", j=4)
            )

        def regroup(engine, mat, h, g, lo=0, hi=HALF):
            if ("gm", mat, h) not in t:
                t["gm", mat, h] = keep.tile([P, 8 * HALF], BF16, name="gm%d%d" % (mat, h), align_bytes=64)
            gm = t["gm", mat, h][:, 4 * HALF * g : 4 * HALF * g + 4 * HALF]
            dst = gm.rearrange("p (c i j) -> p c j i", i=4, j=4)[:, lo // 4 : hi // 4]
            src = t["raw", mat, h, g].rearrange("p j (c i) -> p c j i", i=4)[:, lo // 4 : hi // 4]
            if engine == "v":
                nc.vector.tensor_copy(out=dst, in_=src)
            elif engine == "g":
                nc.gpsimd.tensor_scalar(
                    out=gm[:, 4 * lo : 4 * hi].rearrange("p (c j) -> p c j", j=4),
                    in0=t["raw", mat, h, g][:, :, lo:hi].rearrange("p j c -> p c j"),
                    scalar1=1.0,
                    scalar2=0.0,
                    op0=MULT,
                    op1=ADD,
                )
            else:
                nc.scalar.copy(out=dst, in_=src)

        def quantise(key, label, width, src):
            t[("c",) + key] = keep.tile([P, width], U32, name="c_" + label, align_bytes=64)
            t[("s",) + key] = keep.tile([P, width], U8, name="s_" + label, align_bytes=64)
            nc.vector.quantize_mx(out=t[("c",) + key][:].bitcast(FP8X4), scales=t[("s",) + key][:], in_=src)

        def qm(mat, h, *gs):
            width = HALF * len(gs)
            lo = 4 * HALF * gs[0]
            key = ("m", mat, h, gs)
            quantise(key, "m%d%d%d" % (mat, h, gs[0]), width, t["gm", mat, h][:, lo : lo + 4 * width])
            for n, g in enumerate(gs):
                for kind in ("c", "s"):
                    t[kind, "m", mat, h, g] = t[(kind,) + key][:, HALF * n : HALF * n + HALF]

        def tx(i):
            xw = t["xp", i][:].bitcast(F32)
            for mi in range(2):
                tp = bank()
                t["tpx", i, mi] = tp
                for j in range(4):
                    lo = HALF * mi + 2 * P * (j // 2) + j % 2
                    nc.tensor.transpose(tp[:, P * j : P * j + P], xw[:, lo : lo + 2 * P - 1 : 2], ident[:])

        def cx(i):
            t["gx", i] = keep.tile([P, 2 * D], BF16, name="gx%d" % i, align_bytes=64)
            gw = t["gx", i][:].bitcast(F32)
            for mi in range(2):
                nc.scalar.copy(
                    out=gw[:, HALF * mi : HALF * mi + HALF].rearrange("p (g b u) -> p g b u", g=2, u=2),
                    in_=t["tpx", i, mi][:].rearrange("p (g u b) -> p g b u", g=2, u=2),
                )

        def qx(i):
            quantise(("x", i), "x%d" % i, HALF, t["gx", i][:])

        def mx(stage_no, i, h):
            for mi in range(2):
                acc = bank()
                t["acc", stage_no, i, h, mi] = acc
                for g in range(2):
                    if stage_no == 1:
                        key = ("x", i)
                        lo = 256 * mi + P * g
                    else:
                        key = ("y", i)
                        lo = 2 * P * g + P * mi
                    nc.tensor.matmul_mx(
                        out=acc[:],
                        lhsT=t[("c",) + key][:, lo : lo + P].bitcast(FP8X4),
                        lhsT_scale=t[("s",) + key][:, lo : lo + P],
                        rhs=t["c", "m", stage_no - 1, h, g].bitcast(FP8X4),
                        rhs_scale=t["s", "m", stage_no - 1, h, g],
                        start=(g == 0),
                        stop=(g == 1),
                    )

        def sum1(i, h):
            for mi in range(2):
                m = 2 * i + mi
                x1 = keep.tile([P, HALF], F32, name="x1_%d_%d" % (m, h))
                t["x1", m, h] = x1
                nc.vector.scalar_tensor_tensor(
                    out=x1[:].rearrange("p (j b) -> p j b", j=4),
                    in0=t["acc", 1, i, h, mi][:].rearrange("p (b j) -> p j b", j=4),
                    scalar=c_bf[:, 2 * m : 2 * m + 1],
                    in1=t["xp", i][:, D * mi + HALF * h : D * mi + HALF * h + HALF].rearrange(
                        "p (b j) -> p j b", j=4
                    ),
                    op0=MULT,
                    op1=ADD,
                )

        def t1(i, h):
            for mi in range(2):
                tp = bank()
                t["tp1", i, h, mi] = tp
                for j in range(4):
                    nc.tensor.transpose(
                        tp[:, P * j : P * j + P], t["x1", 2 * i + mi, h][:, P * j : P * j + P], ident[:]
                    )

        def c1(i, h):
            if h == 0:
                t["gx1", i] = keep.tile([P, 2 * D], BF16, name="gx1_%d" % i, align_bytes=64)
            gx = t["gx1", i][:, D * h : D * h + D]
            for mi in range(2):
                nc.scalar.copy(
                    out=gx[:, HALF * mi : HALF * mi + HALF].rearrange("p (b j) -> p b j", j=4),
                    in_=t["tp1", i, h, mi][:].rearrange("p (j b) -> p b j", j=4),
                )

        def q1(i):
            quantise(("y", i), "y%d" % i, 4 * P, t["gx1", i][:])

        def sum2(i, h):
            for mi in range(2):
                m = 2 * i + mi
                acc = t["acc", 2, i, h, mi]
                c = c_bf[:, 2 * m + 1 : 2 * m + 2]
                res = stage.tile([P, HALF], F32, name="o", tag="o", bufs=16)
                t["res", m, h] = res
                new = res[:].rearrange("p (b j) -> p b j", j=4)
                old = t["x1", m, h][:].rearrange("p (j b) -> p b j", j=4)
                nc.vector.scalar_tensor_tensor(
                    out=new, in0=acc[:].rearrange("p (b j) -> p b j", j=4), scalar=c, in1=old, op0=MULT, op1=ADD
                )

        def st(i, h, mi):
            m = 2 * i + mi
            nc.sync.dma_start(out=ov[:, m, HALF * h : HALF * h + HALF], in_=t["res", m, h][:])

        zeros = keep.tile([P, HALF], BF16, name="zeros")
        nc.gpsimd.memset(zeros[:], 0.0)

        def warm(n):
            for k in range(n):
                w = bank()
                nc.tensor.matmul(w[:], zeros[:, 0:P], zeros[:], start=True, stop=True)

        def rv(*k):
            regroup("v", *k)

        def rg(mat, h, g):
            for lo in range(0, HALF, P):
                regroup("g", mat, h, g, lo, lo + P)

        def rs(*k):
            regroup("s", *k)


        load_m0(0, 0)
        load_x(0)
        load_m0(0, 1)
        load_x(1)
        load_m0(1, 0)
        load_x(2)
        load_m0(1, 1)
        load_x(3)
        load_m1(0)
        load_m1(1)
        warm(6)
        tx(0)
        cx(0)
        warm(2)
        rv(0, 0, 0)
        qm(0, 0, 0)
        rv(0, 0, 1)
        qx(0)
        qm(0, 0, 1)
        tx(1)
        cx(1)
        mx(1, 0, 0)
        rs(0, 1, 0)
        qx(1)
        tx(2)
        mx(1, 1, 0)
        sum1(0, 0)
        rv(0, 1, 1)
        cx(2)
        tx(3)
        cx(3)
        qm(0, 1, 0)
        qm(0, 1, 1)
        sum1(1, 0)
        mx(1, 0, 1)
        mx(1, 1, 1)
        qx(2)
        rg(1, 0, 1)
        rs(1, 0, 0)
        sum1(0, 1)
        t1(0, 0)
        t1(1, 0)
        c1(0, 0)
        c1(1, 0)
        sum1(1, 1)
        qx(3)
        mx(1, 2, 0)
        mx(1, 2, 1)
        rs(1, 1, 0)
        sum1(2, 0)
        t1(0, 1)
        t1(1, 1)
        c1(0, 1)
        c1(1, 1)
        sum1(2, 1)
        mx(1, 3, 0)
        mx(1, 3, 1)
        qm(1, 0, 0, 1)
        sum1(3, 0)
        q1(0)
        q1(1)
        sum1(3, 1)
        rs(1, 1, 1)
        t1(2, 0)
        t1(2, 1)
        c1(2, 0)
        c1(2, 1)
        mx(2, 0, 0)
        mx(2, 1, 0)
        sum2(0, 0)
        st(0, 0, 0)
        st(0, 0, 1)
        qm(1, 1, 0, 1)
        t1(3, 0)
        t1(3, 1)
        c1(3, 0)
        c1(3, 1)
        sum2(1, 0)
        st(1, 0, 0)
        st(1, 0, 1)
        mx(2, 0, 1)
        q1(2)
        sum2(0, 1)
        st(0, 1, 0)
        st(0, 1, 1)
        mx(2, 1, 1)
        sum2(1, 1)
        st(1, 1, 0)
        st(1, 1, 1)
        q1(3)
        mx(2, 2, 0)
        sum2(2, 0)
        st(2, 0, 0)
        st(2, 0, 1)
        mx(2, 2, 1)
        sum2(2, 1)
        st(2, 1, 0)
        st(2, 1, 1)
        mx(2, 3, 0)
        sum2(3, 0)
        st(3, 0, 0)
        st(3, 0, 1)
        mx(2, 3, 1)
        sum2(3, 1)
        st(3, 1, 0)
        st(3, 1, 1)
